import numpy as np
import ml_dtypes

BF16 = ml_dtypes.bfloat16


def bf(x):
    return np.asarray(x, np.float32).astype(BF16)


def f32(x):
    return np.asarray(x, np.float32)


def f64(x):
    return np.asarray(x).astype(np.float64)


def striped(idx):
    return np.tile(idx.reshape(-1, 16).T, (8, 1))


E, H, D, C, S, N = 256, 2, 512, 1024, 256, 512


def setup_inputs():
    center = 0.3 * np.random.standard_normal((D, S))
    u = np.random.uniform(0.2, 1.0, (H, E, S))
    u = u / np.exp(np.mean(np.log(u), axis=1, keepdims=True))
    sign = np.where(np.random.uniform(size=(H, E, S)) < 0.5, -1.0, 1.0)
    table = f32(np.concatenate([center, (u * sign).reshape(D, S)], axis=0))
    box_size = f32(0.7 * np.random.standard_normal((H, S)))
    head_emb = f32(0.3 * np.random.standard_normal((D, N)))
    tail_emb = f32(0.3 * np.random.standard_normal((D, N)))
    return {"table": table, "box_size": box_size, "head_emb": head_emb, "tail_emb": tail_emb, "offs": striped(np.random.permutation(np.tile(np.arange(S), 2))[:N])}


def reference(table, box_size, head_emb, tail_emb, offs):
    idx = offs[:16].T.reshape(-1)
    t = f64(table)
    sz = f64(box_size)
    hd = f64(head_emb)
    tl = f64(tail_emb)
    tc = np.tanh(t[:D])
    scale = np.where(sz > 0.0, 1.0 + sz, np.exp(np.minimum(sz, 0.0)))
    w = np.tanh(np.abs(t[D:]).reshape(H, E, S) * scale[:, None, :]).reshape(D, S)
    bumped = np.tanh(np.concatenate([hd[:E] + tl[E:], tl[:E] + hd[E:]], axis=0))
    cd = np.abs(bumped - tc[:, idx])
    wj = w[:, idx]
    p = wj + 1.0
    kappa = 0.5 * wj * (p - 1.0 / p)
    dist = np.where(cd <= 0.5 * wj, cd / p, cd * p - kappa)
    norm = np.sqrt(np.sum((dist ** 2).reshape(H, E, N), axis=1))
    return -np.sum(norm, axis=0, keepdims=True)

@@ -1,0 +1,110 @@
+import concourse.mybir as mybir
+
+F32 = mybir.dt.float32
+BF16 = mybir.dt.bfloat16
+U16 = mybir.dt.uint16
+FN = mybir.ActivationFunctionType
+ALU = mybir.AluOpType
+
+P = 128
+S = 256
+N = 512
+BLOCKS = 4
+PIECE = 256
+PIECES = N // PIECE
+
+FLOPS = 2 * BLOCKS * P * N
+
+
+def tile_boxe_kernel(tc, table, box_size, head_emb, tail_emb, offs, out):
+    nc = tc.nc
+    with (
+        tc.tile_pool(name="held", bufs=1) as held,
+        tc.tile_pool(name="prep", bufs=2) as prep,
+        tc.tile_pool(name="work", bufs=3) as work,
+        tc.psum_pool(name="psum", bufs=1) as psum,
+    ):
+        offsets = held.tile([P, N // 16], U16, name="offsets")
+        nc.sync.dma_start(offsets[:], offs)
+        size = held.tile([P, 2 * S], F32, name="size")
+        nc.scalar.dma_start(size[:], box_size.rearrange("h s -> (h s)").partition_broadcast(P))
+        centre, width, head, tail = [], [], [], []
+        for b in range(BLOCKS):
+            rows = slice(b * P, (b + 1) * P)
+            other = slice(((b + 2) % BLOCKS) * P, ((b + 2) % BLOCKS + 1) * P)
+            width.append(held.tile([P, S], F32, name=f"width{b}"))
+            nc.scalar.dma_start(width[b][:], table[BLOCKS * P + b * P : BLOCKS * P + (b + 1) * P, :])
+            head.append(held.tile([P, N], F32, name=f"head{b}"))
+            nc.sync.dma_start(head[b][:], head_emb[rows, :])
+            tail.append(held.tile([P, N], F32, name=f"tail{b}"))
+            nc.scalar.dma_start(tail[b][:], tail_emb[other, :])
+            centre.append(held.tile([P, S], F32, name=f"centre{b}"))
+            nc.sync.dma_start(centre[b][:], table[rows, :])
+
+        ones = held.tile([P, 1], BF16, name="ones")
+        nc.vector.memset(ones[:], 1.0)
+
+        below = held.tile([P, 2 * S], F32, name="below")
+        nc.vector.tensor_scalar_min(below[:], size[:], 0.0)
+        nc.scalar.activation(below[:], below[:], FN.Exp)
+        scale = held.tile([P, 2 * S], F32, name="scale")
+        nc.vector.scalar_tensor_tensor(scale[:], size[:], 0.0, below[:], ALU.max, ALU.add)
+
+        tanh_centre, minus_half_w, inv_p, slope_gain, minus_bumped = [], [], [], [], []
+        for b in range(BLOCKS):
+            box = b // 2
+            tanh_centre.append(held.tile([P, S], F32, name=f"tanh_centre{b}"))
+            nc.scalar.activation(tanh_centre[b][:], centre[b][:], FN.Tanh)
+
+            arg = prep.tile([P, S], F32, name="arg")
+            nc.gpsimd.tensor_tensor(arg[:], width[b][:], scale[:, box * S : (box + 1) * S], ALU.mult)
+            nc.scalar.activation(arg[:], arg[:], FN.Abs)
+            w = prep.tile([P, S], F32, name="w")
+            nc.scalar.activation(w[:], arg[:], FN.Tanh)
+            decay = prep.tile([P, S], F32, name="decay")
+            nc.scalar.activation(decay[:], arg[:], FN.Exp, scale=-2.0)
+
+            minus_half_w.append(held.tile([P, S], F32, name=f"minus_half_w{b}"))
+            nc.gpsimd.tensor_scalar_mul(minus_half_w[b][:], w[:], -0.5)
+            inv_p.append(held.tile([P, S], F32, name=f"inv_p{b}"))
+            nc.gpsimd.tensor_scalar(inv_p[b][:], decay[:], 0.5, 0.5, ALU.mult, ALU.add)
+            slope_gain.append(held.tile([P, S], F32, name=f"slope_gain{b}"))
+            nc.vector.scalar_tensor_tensor(slope_gain[b][:], w[:], 1.0, inv_p[b][:], ALU.add, ALU.subtract)
+
+            both = prep.tile([P, N], F32, name="both")
+            nc.gpsimd.tensor_tensor(both[:], head[b][:], tail[b][:], ALU.add)
+            minus_bumped.append(held.tile([P, N], F32, name=f"minus_bumped{b}"))
+            nc.scalar.activation(minus_bumped[b][:], both[:], FN.Tanh, scale=-1.0)
+
+        norm = []
+        for b in range(BLOCKS):
+            box = b // 2
+            squared = work.tile([P, N], BF16, name="squared")
+            for k in range(PIECES):
+                cols = slice(k * PIECE, (k + 1) * PIECE)
+                piece = offsets[:, k * (PIECE // 16) : (k + 1) * (PIECE // 16)]
+                diff = work.tile([P, PIECE], F32, name="diff")
+                nc.vector.tensor_tensor(diff[:], tanh_centre[b][:].indirect(piece), minus_bumped[b][:, cols], ALU.add)
+                cd = work.tile([P, PIECE], F32, name="cd")
+                nc.scalar.activation(cd[:], diff[:], FN.Abs)
+                outside = work.tile([P, PIECE], F32, name="outside")
+                nc.vector.tensor_tensor(outside[:], minus_half_w[b][:].indirect(piece), cd[:], ALU.add)
+                nc.scalar.activation(outside[:], outside[:], FN.Relu)
+                inner = work.tile([P, PIECE], F32, name="inner")
+                nc.vector.tensor_tensor(inner[:], inv_p[b][:].indirect(piece), cd[:], ALU.mult)
+                outer = work.tile([P, PIECE], F32, name="outer")
+                nc.vector.tensor_tensor(outer[:], slope_gain[b][:].indirect(piece), outside[:], ALU.mult)
+                dist = work.tile([P, PIECE], F32, name="dist")
+                nc.gpsimd.tensor_tensor(dist[:], inner[:], outer[:], ALU.add)
+                nc.scalar.activation(squared[:, cols], dist[:], FN.Square)
+
+            if b % 2 == 0:
+                total = psum.tile([1, N], F32, name=f"total{box}")
+            nc.tensor.matmul(total[:], ones[:], squared[:], start=(b % 2 == 0), stop=(b % 2 == 1))
+            if b % 2 == 1:
+                norm.append(held.tile([1, N], F32, name=f"norm{box}"))
+                nc.scalar.activation(norm[box][:], total[:], FN.Sqrt)
+
+        score = held.tile([1, N], F32, name="score")
+        nc.vector.scalar_tensor_tensor(score[:], norm[0][:], -1.0, norm[1][:], ALU.mult, ALU.subtract)
+        nc.sync.dma_start(out, score[:])

@@ -1,4 +1,5 @@
 import concourse.mybir as mybir
+from concourse.masks import make_identity
 
 F32 = mybir.dt.float32
 BF16 = mybir.dt.bfloat16
@@ -12,6 +13,7 @@ N = 512
 BLOCKS = 4
 PIECE = 256
 PIECES = N // PIECE
+UNITS = BLOCKS * PIECES
 
 FLOPS = 2 * BLOCKS * P * N
 
@@ -22,27 +24,30 @@ def tile_boxe_kernel(tc, table, box_size, head_emb, tail_emb, offs, out):
         tc.tile_pool(name="held", bufs=1) as held,
         tc.tile_pool(name="prep", bufs=2) as prep,
         tc.tile_pool(name="work", bufs=3) as work,
-        tc.psum_pool(name="psum", bufs=1) as psum,
+        tc.psum_pool(name="sums", bufs=2) as sums,
+        tc.psum_pool(name="totals", bufs=1) as totals,
     ):
-        offsets = held.tile([P, N // 16], U16, name="offsets")
-        nc.sync.dma_start(offsets[:], offs)
+        by_block = table.rearrange("(t b p) s -> b p t s", t=2, b=BLOCKS, p=P)
         size = held.tile([P, 2 * S], F32, name="size")
         nc.scalar.dma_start(size[:], box_size.rearrange("h s -> (h s)").partition_broadcast(P))
-        centre, width, head, tail = [], [], [], []
+        offsets = held.tile([P, N // 16], U16, name="offsets")
+        raw, head, tail = [], [], []
         for b in range(BLOCKS):
-            rows = slice(b * P, (b + 1) * P)
-            other = slice(((b + 2) % BLOCKS) * P, ((b + 2) % BLOCKS + 1) * P)
-            width.append(held.tile([P, S], F32, name=f"width{b}"))
-            nc.scalar.dma_start(width[b][:], table[BLOCKS * P + b * P : BLOCKS * P + (b + 1) * P, :])
+            first = nc.scalar if b == 0 else nc.sync
+            raw.append(held.tile([P, 2, S], F32, name=f"raw{b}"))
+            first.dma_start(raw[b][:], by_block[b])
             head.append(held.tile([P, N], F32, name=f"head{b}"))
-            nc.sync.dma_start(head[b][:], head_emb[rows, :])
+            nc.sync.dma_start(head[b][:], head_emb[b * P : (b + 1) * P, :])
+            other = (b + 2) % BLOCKS
             tail.append(held.tile([P, N], F32, name=f"tail{b}"))
-            nc.scalar.dma_start(tail[b][:], tail_emb[other, :])
-            centre.append(held.tile([P, S], F32, name=f"centre{b}"))
-            nc.sync.dma_start(centre[b][:], table[rows, :])
+            first.dma_start(tail[b][:], tail_emb[other * P : (other + 1) * P, :])
+            if b == 0:
+                nc.sync.dma_start(offsets[:], offs)
 
         ones = held.tile([P, 1], BF16, name="ones")
         nc.vector.memset(ones[:], 1.0)
+        identity = held.tile([P, P], F32, name="identity")
+        make_identity(nc, identity[:])
 
         below = held.tile([P, 2 * S], F32, name="below")
         nc.vector.tensor_scalar_min(below[:], size[:], 0.0)
@@ -50,60 +55,99 @@ def tile_boxe_kernel(tc, table, box_size, head_emb, tail_emb, offs, out):
         scale = held.tile([P, 2 * S], F32, name="scale")
         nc.vector.scalar_tensor_tensor(scale[:], size[:], 0.0, below[:], ALU.max, ALU.add)
 
-        tanh_centre, minus_half_w, inv_p, slope_gain, minus_bumped = [], [], [], [], []
-        for b in range(BLOCKS):
-            box = b // 2
-            tanh_centre.append(held.tile([P, S], F32, name=f"tanh_centre{b}"))
-            nc.scalar.activation(tanh_centre[b][:], centre[b][:], FN.Tanh)
+        tanh_centre = [held.tile([P, S], F32, name=f"tanh_centre{b}") for b in range(BLOCKS)]
+        minus_half_w = [held.tile([P, S], F32, name=f"minus_half_w{b}") for b in range(BLOCKS)]
+        inv_p = [held.tile([P, S], F32, name=f"inv_p{b}") for b in range(BLOCKS)]
+        slope_gain = [held.tile([P, S], F32, name=f"slope_gain{b}") for b in range(BLOCKS)]
+        minus_bumped = [held.tile([P, N], F32, name=f"minus_bumped{b}") for b in range(BLOCKS)]
+        w = [held.tile([P, S], F32, name=f"w{b}") for b in range(BLOCKS)]
+        decay = [held.tile([P, S], F32, name=f"decay{b}") for b in range(BLOCKS)]
 
+        def prepare_start(b):
+            box = b // 2
+            both = sums.tile([P, N], F32, name="both")
+            nc.tensor.matmul(both[:], identity[:], head[b][:], start=True, stop=False)
+            nc.tensor.matmul(both[:], identity[:], tail[b][:], start=False, stop=True)
             arg = prep.tile([P, S], F32, name="arg")
-            nc.gpsimd.tensor_tensor(arg[:], width[b][:], scale[:, box * S : (box + 1) * S], ALU.mult)
+            nc.gpsimd.tensor_tensor(arg[:], raw[b][:, 1, :], scale[:, box * S : (box + 1) * S], ALU.mult)
+
+            nc.scalar.activation(tanh_centre[b][:], raw[b][:, 0, :], FN.Tanh)
             nc.scalar.activation(arg[:], arg[:], FN.Abs)
-            w = prep.tile([P, S], F32, name="w")
-            nc.scalar.activation(w[:], arg[:], FN.Tanh)
-            decay = prep.tile([P, S], F32, name="decay")
-            nc.scalar.activation(decay[:], arg[:], FN.Exp, scale=-2.0)
-
-            minus_half_w.append(held.tile([P, S], F32, name=f"minus_half_w{b}"))
-            nc.gpsimd.tensor_scalar_mul(minus_half_w[b][:], w[:], -0.5)
-            inv_p.append(held.tile([P, S], F32, name=f"inv_p{b}"))
-            nc.gpsimd.tensor_scalar(inv_p[b][:], decay[:], 0.5, 0.5, ALU.mult, ALU.add)
-            slope_gain.append(held.tile([P, S], F32, name=f"slope_gain{b}"))
-            nc.vector.scalar_tensor_tensor(slope_gain[b][:], w[:], 1.0, inv_p[b][:], ALU.add, ALU.subtract)
-
-            both = prep.tile([P, N], F32, name="both")
-            nc.gpsimd.tensor_tensor(both[:], head[b][:], tail[b][:], ALU.add)
-            minus_bumped.append(held.tile([P, N], F32, name=f"minus_bumped{b}"))
             nc.scalar.activation(minus_bumped[b][:], both[:], FN.Tanh, scale=-1.0)
+            nc.scalar.activation(w[b][:], arg[:], FN.Tanh)
+            nc.scalar.activation(decay[b][:], arg[:], FN.Exp, scale=-2.0)
 
-        norm = []
-        for b in range(BLOCKS):
+        def prepare_finish(b):
+            nc.gpsimd.tensor_scalar_mul(minus_half_w[b][:], w[b][:], -0.5)
+            nc.gpsimd.tensor_scalar(inv_p[b][:], decay[b][:], 0.5, 0.5, ALU.mult, ALU.add)
+
+        cd, outside, dist, squared, total, norm = {}, {}, {}, {}, {}, {}
+
+        def piece_of(u):
+            k = u % PIECES
+            return offsets[:, k * (PIECE // 16) : (k + 1) * (PIECE // 16)]
+
+        def subtract(u):
+            b, k = divmod(u, PIECES)
+            diff = work.tile([P, PIECE], F32, name="diff")
+            nc.vector.tensor_tensor(
+                diff[:], tanh_centre[b][:].indirect(piece_of(u)), minus_bumped[b][:, k * PIECE : (k + 1) * PIECE], ALU.add
+            )
+            cd[u] = work.tile([P, PIECE], F32, name="cd")
+            nc.scalar.activation(cd[u][:], diff[:], FN.Abs)
+
+        def excess(u):
+            b = u // PIECES
+            outside[u] = work.tile([P, PIECE], F32, name="outside")
+            nc.vector.tensor_tensor(outside[u][:], minus_half_w[b][:].indirect(piece_of(u)), cd[u][:], ALU.add)
+            nc.scalar.activation(outside[u][:], outside[u][:], FN.Relu)
+
+        def products(u):
+            b, k = divmod(u, PIECES)
+            if k == 0:
+                nc.vector.scalar_tensor_tensor(slope_gain[b][:], w[b][:], 1.0, inv_p[b][:], ALU.add, ALU.subtract)
+            inner = work.tile([P, PIECE], F32, name="inner")
+            nc.vector.tensor_tensor(inner[:], inv_p[b][:].indirect(piece_of(u)), cd[u][:], ALU.mult)
+            outer = work.tile([P, PIECE], F32, name="outer")
+            nc.vector.tensor_tensor(outer[:], slope_gain[b][:].indirect(piece_of(u)), outside[u][:], ALU.mult)
+            dist[u] = work.tile([P, PIECE], F32, name="dist")
+            nc.gpsimd.tensor_tensor(dist[u][:], inner[:], outer[:], ALU.add)
+
+        def reduce_rows(u):
+            b, k = divmod(u, PIECES)
             box = b // 2
-            squared = work.tile([P, N], BF16, name="squared")
-            for k in range(PIECES):
-                cols = slice(k * PIECE, (k + 1) * PIECE)
-                piece = offsets[:, k * (PIECE // 16) : (k + 1) * (PIECE // 16)]
-                diff = work.tile([P, PIECE], F32, name="diff")
-                nc.vector.tensor_tensor(diff[:], tanh_centre[b][:].indirect(piece), minus_bumped[b][:, cols], ALU.add)
-                cd = work.tile([P, PIECE], F32, name="cd")
-                nc.scalar.activation(cd[:], diff[:], FN.Abs)
-                outside = work.tile([P, PIECE], F32, name="outside")
-                nc.vector.tensor_tensor(outside[:], minus_half_w[b][:].indirect(piece), cd[:], ALU.add)
-                nc.scalar.activation(outside[:], outside[:], FN.Relu)
-                inner = work.tile([P, PIECE], F32, name="inner")
-                nc.vector.tensor_tensor(inner[:], inv_p[b][:].indirect(piece), cd[:], ALU.mult)
-                outer = work.tile([P, PIECE], F32, name="outer")
-                nc.vector.tensor_tensor(outer[:], slope_gain[b][:].indirect(piece), outside[:], ALU.mult)
-                dist = work.tile([P, PIECE], F32, name="dist")
-                nc.gpsimd.tensor_tensor(dist[:], inner[:], outer[:], ALU.add)
-                nc.scalar.activation(squared[:, cols], dist[:], FN.Square)
+            if k == 0:
+                squared[b] = work.tile([P, N], BF16, name="squared")
+            nc.scalar.activation(squared[b][:, k * PIECE : (k + 1) * PIECE], dist[u][:], FN.Square)
+            if k == PIECES - 1:
+                if b % 2 == 0:
+                    total[box] = totals.tile([1, N], F32, name=f"total{box}")
+                nc.tensor.matmul(total[box][:], ones[:], squared[b][:], start=(b % 2 == 0), stop=(b % 2 == 1))
 
-            if b % 2 == 0:
-                total = psum.tile([1, N], F32, name=f"total{box}")
-            nc.tensor.matmul(total[:], ones[:], squared[:], start=(b % 2 == 0), stop=(b % 2 == 1))
-            if b % 2 == 1:
-                norm.append(held.tile([1, N], F32, name=f"norm{box}"))
-                nc.scalar.activation(norm[box][:], total[:], FN.Sqrt)
+        def root(box):
+            norm[box] = held.tile([1, N], F32, name=f"norm{box}")
+            nc.scalar.activation(norm[box][:], total[box][:], FN.Sqrt)
+
+        prepare_start(0)
+        prepare_finish(0)
+        subtract(0)
+        for u in range(UNITS):
+            b, k = divmod(u, PIECES)
+            excess(u)
+            if u > 0:
+                reduce_rows(u - 1)
+            if u + 1 < UNITS:
+                subtract(u + 1)
+            if b + 1 < BLOCKS:
+                if k == 0:
+                    prepare_start(b + 1)
+                else:
+                    prepare_finish(b + 1)
+            elif k == 0:
+                root(0)
+            products(u)
+        reduce_rows(UNITS - 1)
+        root(1)
 
         score = held.tile([1, N], F32, name="score")
         nc.vector.scalar_tensor_tensor(score[:], norm[0][:], -1.0, norm[1][:], ALU.mult, ALU.subtract)

@@ -13,7 +13,6 @@ N = 512
 BLOCKS = 4
 PIECE = 256
 PIECES = N // PIECE
-UNITS = BLOCKS * PIECES
 
 FLOPS = 2 * BLOCKS * P * N
 
@@ -22,27 +21,23 @@ def tile_boxe_kernel(tc, table, box_size, head_emb, tail_emb, offs, out):
     nc = tc.nc
     with (
         tc.tile_pool(name="held", bufs=1) as held,
-        tc.tile_pool(name="prep", bufs=2) as prep,
-        tc.tile_pool(name="work", bufs=3) as work,
-        tc.psum_pool(name="sums", bufs=2) as sums,
-        tc.psum_pool(name="totals", bufs=1) as totals,
+        tc.tile_pool(name="work", bufs=4) as work,
+        tc.psum_pool(name="sums", bufs=1) as sums,
     ):
         by_block = table.rearrange("(t b p) s -> b p t s", t=2, b=BLOCKS, p=P)
         size = held.tile([P, 2 * S], F32, name="size")
         nc.scalar.dma_start(size[:], box_size.rearrange("h s -> (h s)").partition_broadcast(P))
         offsets = held.tile([P, N // 16], U16, name="offsets")
+        nc.sync.dma_start(offsets[:], offs)
         raw, head, tail = [], [], []
         for b in range(BLOCKS):
-            first = nc.scalar if b == 0 else nc.sync
             raw.append(held.tile([P, 2, S], F32, name=f"raw{b}"))
-            first.dma_start(raw[b][:], by_block[b])
+            nc.sync.dma_start(raw[b][:], by_block[b])
             head.append(held.tile([P, N], F32, name=f"head{b}"))
             nc.sync.dma_start(head[b][:], head_emb[b * P : (b + 1) * P, :])
             other = (b + 2) % BLOCKS
             tail.append(held.tile([P, N], F32, name=f"tail{b}"))
-            first.dma_start(tail[b][:], tail_emb[other * P : (other + 1) * P, :])
-            if b == 0:
-                nc.sync.dma_start(offsets[:], offs)
+            nc.sync.dma_start(tail[b][:], tail_emb[other * P : (other + 1) * P, :])
 
         ones = held.tile([P, 1], BF16, name="ones")
         nc.vector.memset(ones[:], 1.0)
@@ -55,100 +50,67 @@ def tile_boxe_kernel(tc, table, box_size, head_emb, tail_emb, offs, out):
         scale = held.tile([P, 2 * S], F32, name="scale")
         nc.vector.scalar_tensor_tensor(scale[:], size[:], 0.0, below[:], ALU.max, ALU.add)
 
-        tanh_centre = [held.tile([P, S], F32, name=f"tanh_centre{b}") for b in range(BLOCKS)]
-        minus_half_w = [held.tile([P, S], F32, name=f"minus_half_w{b}") for b in range(BLOCKS)]
-        inv_p = [held.tile([P, S], F32, name=f"inv_p{b}") for b in range(BLOCKS)]
-        slope_gain = [held.tile([P, S], F32, name=f"slope_gain{b}") for b in range(BLOCKS)]
-        minus_bumped = [held.tile([P, N], F32, name=f"minus_bumped{b}") for b in range(BLOCKS)]
-        w = [held.tile([P, S], F32, name=f"w{b}") for b in range(BLOCKS)]
-        decay = [held.tile([P, S], F32, name=f"decay{b}") for b in range(BLOCKS)]
+        tanh_centre, minus_half_w, inv_p, slope_gain, minus_bumped = {}, {}, {}, {}, {}
 
-        def prepare_start(b):
+        def prepare(b):
             box = b // 2
-            both = sums.tile([P, N], F32, name="both")
-            nc.tensor.matmul(both[:], identity[:], head[b][:], start=True, stop=False)
-            nc.tensor.matmul(both[:], identity[:], tail[b][:], start=False, stop=True)
-            arg = prep.tile([P, S], F32, name="arg")
-            nc.gpsimd.tensor_tensor(arg[:], raw[b][:, 1, :], scale[:, box * S : (box + 1) * S], ALU.mult)
-
-            nc.scalar.activation(tanh_centre[b][:], raw[b][:, 0, :], FN.Tanh)
-            nc.scalar.activation(arg[:], arg[:], FN.Abs)
+            if b == 0:
+                both = held.tile([P, N], F32, name="both0")
+                nc.vector.tensor_tensor(both[:], head[b][:], tail[b][:], ALU.add)
+            else:
+                both = sums.tile([P, N], F32, name=f"both{b}")
+                nc.tensor.matmul(both[:], identity[:], head[b][:], start=True, stop=False)
+                nc.tensor.matmul(both[:], identity[:], tail[b][:], start=False, stop=True)
+            minus_bumped[b] = held.tile([P, N], F32, name=f"minus_bumped{b}")
             nc.scalar.activation(minus_bumped[b][:], both[:], FN.Tanh, scale=-1.0)
-            nc.scalar.activation(w[b][:], arg[:], FN.Tanh)
-            nc.scalar.activation(decay[b][:], arg[:], FN.Exp, scale=-2.0)
+            tanh_centre[b] = held.tile([P, S], F32, name=f"tanh_centre{b}")
+            nc.scalar.activation(tanh_centre[b][:], raw[b][:, 0, :], FN.Tanh)
 
-        def prepare_finish(b):
-            nc.gpsimd.tensor_scalar_mul(minus_half_w[b][:], w[b][:], -0.5)
-            nc.gpsimd.tensor_scalar(inv_p[b][:], decay[b][:], 0.5, 0.5, ALU.mult, ALU.add)
+            arg = held.tile([P, S], F32, name=f"arg{b}")
+            nc.vector.tensor_tensor(arg[:], raw[b][:, 1, :], scale[:, box * S : (box + 1) * S], ALU.mult)
+            nc.scalar.activation(arg[:], arg[:], FN.Abs)
+            w = held.tile([P, S], F32, name=f"w{b}")
+            nc.scalar.activation(w[:], arg[:], FN.Tanh)
+            minus_half_w[b] = held.tile([P, S], F32, name=f"minus_half_w{b}")
+            nc.scalar.activation(minus_half_w[b][:], w[:], FN.Copy, scale=-0.5)
+            decay = held.tile([P, S], F32, name=f"decay{b}")
+            nc.scalar.activation(decay[:], arg[:], FN.Exp, scale=-2.0)
+            inv_p[b] = held.tile([P, S], F32, name=f"inv_p{b}")
+            nc.scalar.activation(inv_p[b][:], decay[:], FN.Copy, bias=0.5, scale=0.5)
+            slope_gain[b] = held.tile([P, S], F32, name=f"slope_gain{b}")
+            nc.vector.scalar_tensor_tensor(slope_gain[b][:], w[:], 1.0, inv_p[b][:], ALU.add, ALU.subtract)
 
-        cd, outside, dist, squared, total, norm = {}, {}, {}, {}, {}, {}
-
-        def piece_of(u):
-            k = u % PIECES
-            return offsets[:, k * (PIECE // 16) : (k + 1) * (PIECE // 16)]
-
-        def subtract(u):
-            b, k = divmod(u, PIECES)
+        def look_up(b, k, squared):
+            cols = slice(k * PIECE, (k + 1) * PIECE)
+            piece = offsets[:, k * (PIECE // 16) : (k + 1) * (PIECE // 16)]
             diff = work.tile([P, PIECE], F32, name="diff")
-            nc.vector.tensor_tensor(
-                diff[:], tanh_centre[b][:].indirect(piece_of(u)), minus_bumped[b][:, k * PIECE : (k + 1) * PIECE], ALU.add
-            )
-            cd[u] = work.tile([P, PIECE], F32, name="cd")
-            nc.scalar.activation(cd[u][:], diff[:], FN.Abs)
-
-        def excess(u):
-            b = u // PIECES
-            outside[u] = work.tile([P, PIECE], F32, name="outside")
-            nc.vector.tensor_tensor(outside[u][:], minus_half_w[b][:].indirect(piece_of(u)), cd[u][:], ALU.add)
-            nc.scalar.activation(outside[u][:], outside[u][:], FN.Relu)
-
-        def products(u):
-            b, k = divmod(u, PIECES)
-            if k == 0:
-                nc.vector.scalar_tensor_tensor(slope_gain[b][:], w[b][:], 1.0, inv_p[b][:], ALU.add, ALU.subtract)
+            nc.vector.tensor_tensor(diff[:], tanh_centre[b][:].indirect(piece), minus_bumped[b][:, cols], ALU.add)
+            cd = work.tile([P, PIECE], F32, name="cd")
+            nc.scalar.activation(cd[:], diff[:], FN.Abs)
+            outside = work.tile([P, PIECE], F32, name="outside")
+            nc.vector.tensor_tensor(outside[:], minus_half_w[b][:].indirect(piece), cd[:], ALU.add)
+            nc.scalar.activation(outside[:], outside[:], FN.Relu)
             inner = work.tile([P, PIECE], F32, name="inner")
-            nc.vector.tensor_tensor(inner[:], inv_p[b][:].indirect(piece_of(u)), cd[u][:], ALU.mult)
+            nc.vector.tensor_tensor(inner[:], inv_p[b][:].indirect(piece), cd[:], ALU.mult)
             outer = work.tile([P, PIECE], F32, name="outer")
-            nc.vector.tensor_tensor(outer[:], slope_gain[b][:].indirect(piece_of(u)), outside[u][:], ALU.mult)
-            dist[u] = work.tile([P, PIECE], F32, name="dist")
-            nc.gpsimd.tensor_tensor(dist[u][:], inner[:], outer[:], ALU.add)
+            nc.vector.tensor_tensor(outer[:], slope_gain[b][:].indirect(piece), outside[:], ALU.mult)
+            dist = work.tile([P, PIECE], F32, name="dist")
+            nc.vector.tensor_tensor(dist[:], inner[:], outer[:], ALU.add)
+            nc.scalar.activation(squared[:, cols], dist[:], FN.Square)
 
-        def reduce_rows(u):
-            b, k = divmod(u, PIECES)
-            box = b // 2
-            if k == 0:
-                squared[b] = work.tile([P, N], BF16, name="squared")
-            nc.scalar.activation(squared[b][:, k * PIECE : (k + 1) * PIECE], dist[u][:], FN.Square)
-            if k == PIECES - 1:
-                if b % 2 == 0:
-                    total[box] = totals.tile([1, N], F32, name=f"total{box}")
-                nc.tensor.matmul(total[box][:], ones[:], squared[b][:], start=(b % 2 == 0), stop=(b % 2 == 1))
-
-        def root(box):
-            norm[box] = held.tile([1, N], F32, name=f"norm{box}")
-            nc.scalar.activation(norm[box][:], total[box][:], FN.Sqrt)
-
-        prepare_start(0)
-        prepare_finish(0)
-        subtract(0)
-        for u in range(UNITS):
-            b, k = divmod(u, PIECES)
-            excess(u)
-            if u > 0:
-                reduce_rows(u - 1)
-            if u + 1 < UNITS:
-                subtract(u + 1)
+        total = [sums.tile([1, N], F32, name=f"total{box}") for box in range(2)]
+        prepare(0)
+        for b in range(BLOCKS):
             if b + 1 < BLOCKS:
-                if k == 0:
-                    prepare_start(b + 1)
-                else:
-                    prepare_finish(b + 1)
-            elif k == 0:
-                root(0)
-            products(u)
-        reduce_rows(UNITS - 1)
-        root(1)
+                prepare(b + 1)
+            squared = work.tile([P, N], BF16, name="squared")
+            for k in range(PIECES):
+                look_up(b, k, squared)
+            nc.tensor.matmul(total[b // 2][:], ones[:], squared[:], start=(b % 2 == 0), stop=(b % 2 == 1))
 
+        norm = [held.tile([1, N], F32, name=f"norm{box}") for box in range(2)]
+        for box in range(2):
+            nc.scalar.activation(norm[box][:], total[box][:], FN.Sqrt)
         score = held.tile([1, N], F32, name="score")
         nc.vector.scalar_tensor_tensor(score[:], norm[0][:], -1.0, norm[1][:], ALU.mult, ALU.subtract)
         nc.sync.dma_start(out, score[:])

@@ -13,6 +13,7 @@ N = 512
 BLOCKS = 4
 PIECE = 256
 PIECES = N // PIECE
+ORDER = (0, 2, 1, 3)
 
 FLOPS = 2 * BLOCKS * P * N
 
@@ -23,20 +24,21 @@ def tile_boxe_kernel(tc, table, box_size, head_emb, tail_emb, offs, out):
         tc.tile_pool(name="held", bufs=1) as held,
         tc.tile_pool(name="work", bufs=4) as work,
         tc.psum_pool(name="sums", bufs=1) as sums,
+        tc.psum_pool(name="dists", bufs=2) as dists,
     ):
         by_block = table.rearrange("(t b p) s -> b p t s", t=2, b=BLOCKS, p=P)
         size = held.tile([P, 2 * S], F32, name="size")
         nc.scalar.dma_start(size[:], box_size.rearrange("h s -> (h s)").partition_broadcast(P))
         offsets = held.tile([P, N // 16], U16, name="offsets")
         nc.sync.dma_start(offsets[:], offs)
-        raw, head, tail = [], [], []
-        for b in range(BLOCKS):
-            raw.append(held.tile([P, 2, S], F32, name=f"raw{b}"))
+        raw, head, tail = {}, {}, {}
+        for b in ORDER:
+            raw[b] = held.tile([P, 2, S], F32, name=f"raw{b}")
             nc.sync.dma_start(raw[b][:], by_block[b])
-            head.append(held.tile([P, N], F32, name=f"head{b}"))
+            head[b] = held.tile([P, N], F32, name=f"head{b}")
             nc.sync.dma_start(head[b][:], head_emb[b * P : (b + 1) * P, :])
             other = (b + 2) % BLOCKS
-            tail.append(held.tile([P, N], F32, name=f"tail{b}"))
+            tail[b] = held.tile([P, N], F32, name=f"tail{b}")
             nc.sync.dma_start(tail[b][:], tail_emb[other * P : (other + 1) * P, :])
 
         ones = held.tile([P, 1], BF16, name="ones")
@@ -94,15 +96,16 @@ def tile_boxe_kernel(tc, table, box_size, head_emb, tail_emb, offs, out):
             nc.vector.tensor_tensor(inner[:], inv_p[b][:].indirect(piece), cd[:], ALU.mult)
             outer = work.tile([P, PIECE], F32, name="outer")
             nc.vector.tensor_tensor(outer[:], slope_gain[b][:].indirect(piece), outside[:], ALU.mult)
-            dist = work.tile([P, PIECE], F32, name="dist")
-            nc.vector.tensor_tensor(dist[:], inner[:], outer[:], ALU.add)
+            dist = dists.tile([P, PIECE], F32, name="dist")
+            nc.tensor.matmul(dist[:], identity[:], inner[:], start=True, stop=False)
+            nc.tensor.matmul(dist[:], identity[:], outer[:], start=False, stop=True)
             nc.scalar.activation(squared[:, cols], dist[:], FN.Square)
 
         total = [sums.tile([1, N], F32, name=f"total{box}") for box in range(2)]
-        prepare(0)
-        for b in range(BLOCKS):
-            if b + 1 < BLOCKS:
-                prepare(b + 1)
+        prepare(ORDER[0])
+        for turn, b in enumerate(ORDER):
+            if turn + 1 < BLOCKS:
+                prepare(ORDER[turn + 1])
             squared = work.tile([P, N], BF16, name="squared")
             for k in range(PIECES):
                 look_up(b, k, squared)

@@ -14,6 +14,8 @@ BLOCKS = 4
 PIECE = 256
 PIECES = N // PIECE
 ORDER = (0, 2, 1, 3)
+ROWS = 4
+CHUNK = N // ROWS
 
 FLOPS = 2 * BLOCKS * P * N
 
@@ -41,8 +43,10 @@ def tile_boxe_kernel(tc, table, box_size, head_emb, tail_emb, offs, out):
             tail[b] = held.tile([P, N], F32, name=f"tail{b}")
             nc.sync.dma_start(tail[b][:], tail_emb[other * P : (other + 1) * P, :])
 
-        ones = held.tile([P, 1], BF16, name="ones")
-        nc.vector.memset(ones[:], 1.0)
+        ones_to = held.tile([P, ROWS, ROWS], BF16, name="ones_to")
+        nc.vector.memset(ones_to[:], 0.0)
+        for q in range(ROWS):
+            nc.vector.memset(ones_to[:, q, q : q + 1], 1.0)
         identity = held.tile([P, P], F32, name="identity")
         make_identity(nc, identity[:])
 
@@ -101,7 +105,7 @@ def tile_boxe_kernel(tc, table, box_size, head_emb, tail_emb, offs, out):
             nc.tensor.matmul(dist[:], identity[:], outer[:], start=False, stop=True)
             nc.scalar.activation(squared[:, cols], dist[:], FN.Square)
 
-        total = [sums.tile([1, N], F32, name=f"total{box}") for box in range(2)]
+        total = [sums.tile([ROWS, CHUNK], F32, name=f"total{box}") for box in range(2)]
         prepare(ORDER[0])
         for turn, b in enumerate(ORDER):
             if turn + 1 < BLOCKS:
@@ -109,11 +113,18 @@ def tile_boxe_kernel(tc, table, box_size, head_emb, tail_emb, offs, out):
             squared = work.tile([P, N], BF16, name="squared")
             for k in range(PIECES):
                 look_up(b, k, squared)
-            nc.tensor.matmul(total[b // 2][:], ones[:], squared[:], start=(b % 2 == 0), stop=(b % 2 == 1))
+            for q in range(ROWS):
+                nc.tensor.matmul(
+                    total[b // 2][:],
+                    ones_to[:, q, :],
+                    squared[:, q * CHUNK : (q + 1) * CHUNK],
+                    start=(b % 2 == 0 and q == 0),
+                    stop=(b % 2 == 1 and q == ROWS - 1),
+                )
 
-        norm = [held.tile([1, N], F32, name=f"norm{box}") for box in range(2)]
+        norm = [held.tile([ROWS, CHUNK], F32, name=f"norm{box}") for box in range(2)]
         for box in range(2):
             nc.scalar.activation(norm[box][:], total[box][:], FN.Sqrt)
-        score = held.tile([1, N], F32, name="score")
+        score = held.tile([ROWS, CHUNK], F32, name="score")
         nc.vector.scalar_tensor_tensor(score[:], norm[0][:], -1.0, norm[1][:], ALU.mult, ALU.subtract)
-        nc.sync.dma_start(out, score[:])
+        nc.sync.dma_start(out.rearrange("o (q n) -> (o q) n", q=ROWS), score[:])

@@ -14,6 +14,7 @@ BLOCKS = 4
 PIECE = 256
 PIECES = N // PIECE
 ORDER = (0, 2, 1, 3)
+UNITS = BLOCKS * PIECES
 ROWS = 4
 CHUNK = N // ROWS
 
@@ -24,107 +25,182 @@ def tile_boxe_kernel(tc, table, box_size, head_emb, tail_emb, offs, out):
     nc = tc.nc
     with (
         tc.tile_pool(name="held", bufs=1) as held,
-        tc.tile_pool(name="work", bufs=4) as work,
-        tc.psum_pool(name="sums", bufs=1) as sums,
-        tc.psum_pool(name="dists", bufs=2) as dists,
+        tc.psum_pool(name="totals", bufs=1) as totals,
+        tc.psum_pool(name="sums", bufs=2) as sums,
+        tc.psum_pool(name="dists", bufs=4) as dists,
     ):
-        by_block = table.rearrange("(t b p) s -> b p t s", t=2, b=BLOCKS, p=P)
-        size = held.tile([P, 2 * S], F32, name="size")
-        nc.scalar.dma_start(size[:], box_size.rearrange("h s -> (h s)").partition_broadcast(P))
         offsets = held.tile([P, N // 16], U16, name="offsets")
         nc.sync.dma_start(offsets[:], offs)
-        raw, head, tail = {}, {}, {}
-        for b in ORDER:
-            raw[b] = held.tile([P, 2, S], F32, name=f"raw{b}")
-            nc.sync.dma_start(raw[b][:], by_block[b])
-            head[b] = held.tile([P, N], F32, name=f"head{b}")
-            nc.sync.dma_start(head[b][:], head_emb[b * P : (b + 1) * P, :])
+        size = [held.tile([P, S], F32, name=f"size{box}") for box in range(2)]
+        width = [held.tile([P, S], F32, name=f"width{b}") for b in range(BLOCKS)]
+        centre = [held.tile([P, S], F32, name=f"centre{b}") for b in range(BLOCKS)]
+        head = [held.tile([P, N], F32, name=f"head{b}") for b in range(BLOCKS)]
+        tail = [held.tile([P, N], F32, name=f"tail{b}") for b in range(BLOCKS)]
+
+        def load_rows(tile_ap, rows, b, cols):
+            nc.sync.dma_start(tile_ap[:, cols], rows[b * P : (b + 1) * P, cols])
+
+        for turn, b in enumerate(ORDER):
             other = (b + 2) % BLOCKS
-            tail[b] = held.tile([P, N], F32, name=f"tail{b}")
-            nc.sync.dma_start(tail[b][:], tail_emb[other * P : (other + 1) * P, :])
+            if turn == 0:
+                nc.scalar.dma_start(size[0][:], box_size[0].partition_broadcast(P))
+                load_rows(width[b], table, BLOCKS + b, slice(0, S))
+                load_rows(centre[b], table, b, slice(0, S))
+                for k in range(PIECES):
+                    load_rows(head[b], head_emb, b, slice(k * PIECE, (k + 1) * PIECE))
+                    nc.sync.dma_start(
+                        tail[b][:, k * PIECE : (k + 1) * PIECE],
+                        tail_emb[other * P : (other + 1) * P, k * PIECE : (k + 1) * PIECE],
+                    )
+            else:
+                if turn == 1:
+                    nc.sync.dma_start(size[1][:], box_size[1].partition_broadcast(P))
+                load_rows(centre[b], table, b, slice(0, S))
+                load_rows(head[b], head_emb, b, slice(0, N))
+                nc.sync.dma_start(tail[b][:], tail_emb[other * P : (other + 1) * P, :])
+                load_rows(width[b], table, BLOCKS + b, slice(0, S))
 
         ones_to = held.tile([P, ROWS, ROWS], BF16, name="ones_to")
-        nc.vector.memset(ones_to[:], 0.0)
+        nc.gpsimd.memset(ones_to[:], 0.0)
         for q in range(ROWS):
-            nc.vector.memset(ones_to[:, q, q : q + 1], 1.0)
+            nc.gpsimd.memset(ones_to[:, q, q : q + 1], 1.0)
         identity = held.tile([P, P], F32, name="identity")
         make_identity(nc, identity[:])
+        minus_identity = held.tile([P, P], F32, name="minus_identity")
+        nc.gpsimd.tensor_scalar(minus_identity[:], identity[:], -1.0, None, ALU.mult)
 
-        below = held.tile([P, 2 * S], F32, name="below")
-        nc.vector.tensor_scalar_min(below[:], size[:], 0.0)
-        nc.scalar.activation(below[:], below[:], FN.Exp)
-        scale = held.tile([P, 2 * S], F32, name="scale")
-        nc.vector.scalar_tensor_tensor(scale[:], size[:], 0.0, below[:], ALU.max, ALU.add)
+        below, scale, abs_width, tanh_centre, minus_bumped = {}, {}, {}, {}, {}
+        minus_w, inv_p, minus_gain = {}, {}, {}
 
-        tanh_centre, minus_half_w, inv_p, slope_gain, minus_bumped = {}, {}, {}, {}, {}
+        def start_scale(box):
+            below[box] = held.tile([P, S], F32, name=f"below{box}")
+            nc.vector.tensor_scalar_min(below[box][:], size[box][:], 0.0)
+            nc.scalar.activation(below[box][:], below[box][:], FN.Exp)
 
-        def prepare(b):
-            box = b // 2
-            if b == 0:
-                both = held.tile([P, N], F32, name="both0")
-                nc.vector.tensor_tensor(both[:], head[b][:], tail[b][:], ALU.add)
-            else:
-                both = sums.tile([P, N], F32, name=f"both{b}")
-                nc.tensor.matmul(both[:], identity[:], head[b][:], start=True, stop=False)
-                nc.tensor.matmul(both[:], identity[:], tail[b][:], start=False, stop=True)
-            minus_bumped[b] = held.tile([P, N], F32, name=f"minus_bumped{b}")
-            nc.scalar.activation(minus_bumped[b][:], both[:], FN.Tanh, scale=-1.0)
+        def end_scale(box):
+            scale[box] = held.tile([P, S], F32, name=f"scale{box}")
+            nc.vector.scalar_tensor_tensor(scale[box][:], size[box][:], 0.0, below[box][:], ALU.max, ALU.add)
+
+        def of_table_alone(b):
+            abs_width[b] = held.tile([P, S], F32, name=f"abs_width{b}")
+            nc.scalar.activation(abs_width[b][:], width[b][:], FN.Abs)
             tanh_centre[b] = held.tile([P, S], F32, name=f"tanh_centre{b}")
-            nc.scalar.activation(tanh_centre[b][:], raw[b][:, 0, :], FN.Tanh)
+            nc.scalar.activation(tanh_centre[b][:], centre[b][:], FN.Tanh)
 
+        def bump(u):
+            b, k = ORDER[u // PIECES], u % PIECES
+            cols = slice(k * PIECE, (k + 1) * PIECE)
+            if u < PIECES:
+                both = held.tile([P, PIECE], F32, name=f"both{u}")
+                nc.vector.tensor_tensor(both[:], head[b][:, cols], tail[b][:, cols], ALU.add)
+            else:
+                both = sums.tile([P, PIECE], F32, name="both")
+                nc.tensor.matmul(both[:], identity[:], head[b][:, cols], start=True, stop=False)
+                nc.tensor.matmul(both[:], identity[:], tail[b][:, cols], start=False, stop=True)
+            minus_bumped[u] = held.tile([P, PIECE], F32, name=f"minus_bumped{u}")
+            nc.scalar.activation(minus_bumped[u][:], both[:], FN.Tanh, scale=-1.0)
+
+        def widths(b):
             arg = held.tile([P, S], F32, name=f"arg{b}")
-            nc.vector.tensor_tensor(arg[:], raw[b][:, 1, :], scale[:, box * S : (box + 1) * S], ALU.mult)
-            nc.scalar.activation(arg[:], arg[:], FN.Abs)
-            w = held.tile([P, S], F32, name=f"w{b}")
-            nc.scalar.activation(w[:], arg[:], FN.Tanh)
-            minus_half_w[b] = held.tile([P, S], F32, name=f"minus_half_w{b}")
-            nc.scalar.activation(minus_half_w[b][:], w[:], FN.Copy, scale=-0.5)
+            nc.vector.tensor_tensor(arg[:], abs_width[b][:], scale[b // 2][:], ALU.mult)
+            minus_w[b] = held.tile([P, S], F32, name=f"minus_w{b}")
+            nc.scalar.activation(minus_w[b][:], arg[:], FN.Tanh, scale=-1.0)
             decay = held.tile([P, S], F32, name=f"decay{b}")
             nc.scalar.activation(decay[:], arg[:], FN.Exp, scale=-2.0)
             inv_p[b] = held.tile([P, S], F32, name=f"inv_p{b}")
             nc.scalar.activation(inv_p[b][:], decay[:], FN.Copy, bias=0.5, scale=0.5)
-            slope_gain[b] = held.tile([P, S], F32, name=f"slope_gain{b}")
-            nc.vector.scalar_tensor_tensor(slope_gain[b][:], w[:], 1.0, inv_p[b][:], ALU.add, ALU.subtract)
 
-        def look_up(b, k, squared):
-            cols = slice(k * PIECE, (k + 1) * PIECE)
-            piece = offsets[:, k * (PIECE // 16) : (k + 1) * (PIECE // 16)]
-            diff = work.tile([P, PIECE], F32, name="diff")
-            nc.vector.tensor_tensor(diff[:], tanh_centre[b][:].indirect(piece), minus_bumped[b][:, cols], ALU.add)
-            cd = work.tile([P, PIECE], F32, name="cd")
-            nc.scalar.activation(cd[:], diff[:], FN.Abs)
-            outside = work.tile([P, PIECE], F32, name="outside")
-            nc.vector.tensor_tensor(outside[:], minus_half_w[b][:].indirect(piece), cd[:], ALU.add)
-            nc.scalar.activation(outside[:], outside[:], FN.Relu)
-            inner = work.tile([P, PIECE], F32, name="inner")
-            nc.vector.tensor_tensor(inner[:], inv_p[b][:].indirect(piece), cd[:], ALU.mult)
-            outer = work.tile([P, PIECE], F32, name="outer")
-            nc.vector.tensor_tensor(outer[:], slope_gain[b][:].indirect(piece), outside[:], ALU.mult)
-            dist = dists.tile([P, PIECE], F32, name="dist")
-            nc.tensor.matmul(dist[:], identity[:], inner[:], start=True, stop=False)
-            nc.tensor.matmul(dist[:], identity[:], outer[:], start=False, stop=True)
-            nc.scalar.activation(squared[:, cols], dist[:], FN.Square)
+        def gain(b):
+            minus_gain[b] = held.tile([P, S], F32, name=f"minus_gain{b}")
+            nc.vector.scalar_tensor_tensor(minus_gain[b][:], inv_p[b][:], -1.0, minus_w[b][:], ALU.add, ALU.add)
 
-        total = [sums.tile([ROWS, CHUNK], F32, name=f"total{box}") for box in range(2)]
-        prepare(ORDER[0])
-        for turn, b in enumerate(ORDER):
-            if turn + 1 < BLOCKS:
-                prepare(ORDER[turn + 1])
-            squared = work.tile([P, N], BF16, name="squared")
-            for k in range(PIECES):
-                look_up(b, k, squared)
-            for q in range(ROWS):
+        def piece_of(u):
+            k = u % PIECES
+            return offsets[:, k * (PIECE // 16) : (k + 1) * (PIECE // 16)]
+
+        twice_cd, twice_outside, inner, twice_dist, squared = {}, {}, {}, {}, {}
+        total = [totals.tile([ROWS, CHUNK], F32, name=f"total{box}") for box in range(2)]
+        norm = [held.tile([ROWS, CHUNK], F32, name=f"norm{box}") for box in range(2)]
+
+        def first_stage(u):
+            b = ORDER[u // PIECES]
+            diff = held.tile([P, PIECE], F32, name=f"diff{u}")
+            nc.vector.tensor_tensor(diff[:], tanh_centre[b][:].indirect(piece_of(u)), minus_bumped[u][:], ALU.add)
+            twice_cd[u] = held.tile([P, PIECE], F32, name=f"twice_cd{u}")
+            nc.scalar.activation(twice_cd[u][:], diff[:], FN.Abs, scale=2.0)
+
+        def second_stage(u):
+            b = ORDER[u // PIECES]
+            beyond = held.tile([P, PIECE], F32, name=f"beyond{u}")
+            nc.vector.tensor_tensor(beyond[:], minus_w[b][:].indirect(piece_of(u)), twice_cd[u][:], ALU.add)
+            twice_outside[u] = held.tile([P, PIECE], F32, name=f"twice_outside{u}")
+            nc.scalar.activation(twice_outside[u][:], beyond[:], FN.Relu)
+            inner[u] = held.tile([P, PIECE], F32, name=f"inner{u}")
+            nc.vector.tensor_tensor(inner[u][:], inv_p[b][:].indirect(piece_of(u)), twice_cd[u][:], ALU.mult)
+            if u < UNITS - 1:
+                twice_dist[u] = dists.tile([P, PIECE], F32, name="twice_dist")
+                nc.tensor.matmul(twice_dist[u][:], identity[:], inner[u][:], start=True, stop=False)
+
+        def third_stage(u):
+            b = ORDER[u // PIECES]
+            minus_outer = held.tile([P, PIECE], F32, name=f"minus_outer{u}")
+            nc.vector.tensor_tensor(minus_outer[:], minus_gain[b][:].indirect(piece_of(u)), twice_outside[u][:], ALU.mult)
+            squared[u] = held.tile([P, PIECE], BF16, name=f"squared{u}")
+            if u < UNITS - 1:
+                nc.tensor.matmul(twice_dist[u][:], minus_identity[:], minus_outer[:], start=False, stop=True)
+                nc.scalar.activation(squared[u][:], twice_dist[u][:], FN.Square, scale=0.5)
+            else:
+                last = held.tile([P, PIECE], F32, name="last")
+                nc.vector.tensor_tensor(last[:], inner[u][:], minus_outer[:], ALU.subtract)
+                nc.vector.scalar_tensor_tensor(squared[u][:], last[:], 0.25, last[:], ALU.mult, ALU.mult)
+
+        def fourth_stage(u):
+            b, k = ORDER[u // PIECES], u % PIECES
+            box = b // 2
+            for half in range(PIECE // CHUNK):
+                q = k * (PIECE // CHUNK) + half
                 nc.tensor.matmul(
-                    total[b // 2][:],
+                    total[box][:],
                     ones_to[:, q, :],
-                    squared[:, q * CHUNK : (q + 1) * CHUNK],
+                    squared[u][:, half * CHUNK : (half + 1) * CHUNK],
                     start=(b % 2 == 0 and q == 0),
                     stop=(b % 2 == 1 and q == ROWS - 1),
                 )
+            if b % 2 == 1 and k == PIECES - 1:
+                nc.scalar.activation(norm[box][:], total[box][:], FN.Sqrt)
 
-        norm = [held.tile([ROWS, CHUNK], F32, name=f"norm{box}") for box in range(2)]
-        for box in range(2):
-            nc.scalar.activation(norm[box][:], total[box][:], FN.Sqrt)
+        start_scale(0)
+        of_table_alone(ORDER[0])
+        end_scale(0)
+        bump(0)
+        widths(ORDER[0])
+        bump(1)
+
+        for step in range(UNITS + 3):
+            if step < UNITS:
+                first_stage(step)
+            if 0 <= step - 2 < UNITS:
+                third_stage(step - 2)
+            if 0 <= step - 1 < UNITS:
+                second_stage(step - 1)
+            if 0 <= step - 3 < UNITS:
+                fourth_stage(step - 3)
+            turn, k = step // PIECES, step % PIECES
+            if k == 0 and turn < BLOCKS:
+                gain(ORDER[turn])
+            if turn + 1 < BLOCKS:
+                coming = ORDER[turn + 1]
+                if k == 0:
+                    if turn == 0:
+                        start_scale(1)
+                    of_table_alone(coming)
+                    for u in range(PIECES * (turn + 1), PIECES * (turn + 2)):
+                        bump(u)
+                else:
+                    if turn == 0:
+                        end_scale(1)
+                    widths(coming)
+
         score = held.tile([ROWS, CHUNK], F32, name="score")
         nc.vector.scalar_tensor_tensor(score[:], norm[0][:], -1.0, norm[1][:], ALU.mult, ALU.subtract)
         nc.sync.dma_start(out.rearrange("o (q n) -> (o q) n", q=ROWS), score[:])

@@ -31,7 +31,7 @@ def tile_boxe_kernel(tc, table, box_size, head_emb, tail_emb, offs, out):
     ):
         offsets = held.tile([P, N // 16], U16, name="offsets")
         nc.sync.dma_start(offsets[:], offs)
-        size = [held.tile([P, S], F32, name=f"size{box}") for box in range(2)]
+        size = held.tile([P, 2 * S], F32, name="size")
         width = [held.tile([P, S], F32, name=f"width{b}") for b in range(BLOCKS)]
         centre = [held.tile([P, S], F32, name=f"centre{b}") for b in range(BLOCKS)]
         head = [held.tile([P, N], F32, name=f"head{b}") for b in range(BLOCKS)]
@@ -43,7 +43,7 @@ def tile_boxe_kernel(tc, table, box_size, head_emb, tail_emb, offs, out):
         for turn, b in enumerate(ORDER):
             other = (b + 2) % BLOCKS
             if turn == 0:
-                nc.scalar.dma_start(size[0][:], box_size[0].partition_broadcast(P))
+                nc.scalar.dma_start(size[:], box_size.rearrange("h s -> (h s)").partition_broadcast(P))
                 load_rows(width[b], table, BLOCKS + b, slice(0, S))
                 load_rows(centre[b], table, b, slice(0, S))
                 for k in range(PIECES):
@@ -53,8 +53,6 @@ def tile_boxe_kernel(tc, table, box_size, head_emb, tail_emb, offs, out):
                         tail_emb[other * P : (other + 1) * P, k * PIECE : (k + 1) * PIECE],
                     )
             else:
-                if turn == 1:
-                    nc.sync.dma_start(size[1][:], box_size[1].partition_broadcast(P))
                 load_rows(centre[b], table, b, slice(0, S))
                 load_rows(head[b], head_emb, b, slice(0, N))
                 nc.sync.dma_start(tail[b][:], tail_emb[other * P : (other + 1) * P, :])
@@ -69,17 +67,18 @@ def tile_boxe_kernel(tc, table, box_size, head_emb, tail_emb, offs, out):
         minus_identity = held.tile([P, P], F32, name="minus_identity")
         nc.gpsimd.tensor_scalar(minus_identity[:], identity[:], -1.0, None, ALU.mult)
 
-        below, scale, abs_width, tanh_centre, minus_bumped = {}, {}, {}, {}, {}
+        abs_width, tanh_centre, minus_bumped = {}, {}, {}
         minus_w, inv_p, minus_gain = {}, {}, {}
 
-        def start_scale(box):
-            below[box] = held.tile([P, S], F32, name=f"below{box}")
-            nc.vector.tensor_scalar_min(below[box][:], size[box][:], 0.0)
-            nc.scalar.activation(below[box][:], below[box][:], FN.Exp)
+        below = held.tile([P, 2 * S], F32, name="below")
+        scale = held.tile([P, 2 * S], F32, name="scale")
 
-        def end_scale(box):
-            scale[box] = held.tile([P, S], F32, name=f"scale{box}")
-            nc.vector.scalar_tensor_tensor(scale[box][:], size[box][:], 0.0, below[box][:], ALU.max, ALU.add)
+        def start_scale():
+            nc.vector.tensor_scalar_min(below[:], size[:], 0.0)
+            nc.scalar.activation(below[:], below[:], FN.Exp)
+
+        def end_scale():
+            nc.vector.scalar_tensor_tensor(scale[:], size[:], 0.0, below[:], ALU.max, ALU.add)
 
         def of_table_alone(b):
             abs_width[b] = held.tile([P, S], F32, name=f"abs_width{b}")
@@ -102,7 +101,8 @@ def tile_boxe_kernel(tc, table, box_size, head_emb, tail_emb, offs, out):
 
         def widths(b):
             arg = held.tile([P, S], F32, name=f"arg{b}")
-            nc.vector.tensor_tensor(arg[:], abs_width[b][:], scale[b // 2][:], ALU.mult)
+            box = b // 2
+            nc.vector.tensor_tensor(arg[:], abs_width[b][:], scale[:, box * S : (box + 1) * S], ALU.mult)
             minus_w[b] = held.tile([P, S], F32, name=f"minus_w{b}")
             nc.scalar.activation(minus_w[b][:], arg[:], FN.Tanh, scale=-1.0)
             decay = held.tile([P, S], F32, name=f"decay{b}")
@@ -169,9 +169,9 @@ def tile_boxe_kernel(tc, table, box_size, head_emb, tail_emb, offs, out):
             if b % 2 == 1 and k == PIECES - 1:
                 nc.scalar.activation(norm[box][:], total[box][:], FN.Sqrt)
 
-        start_scale(0)
+        start_scale()
         of_table_alone(ORDER[0])
-        end_scale(0)
+        end_scale()
         bump(0)
         widths(ORDER[0])
         bump(1)
@@ -191,14 +191,10 @@ def tile_boxe_kernel(tc, table, box_size, head_emb, tail_emb, offs, out):
             if turn + 1 < BLOCKS:
                 coming = ORDER[turn + 1]
                 if k == 0:
-                    if turn == 0:
-                        start_scale(1)
                     of_table_alone(coming)
                     for u in range(PIECES * (turn + 1), PIECES * (turn + 2)):
                         bump(u)
                 else:
-                    if turn == 0:
-                        end_scale(1)
                     widths(coming)
 
         score = held.tile([ROWS, CHUNK], F32, name="score")

@@ -32,20 +32,23 @@ def tile_boxe_kernel(tc, table, box_size, head_emb, tail_emb, offs, out):
         offsets = held.tile([P, N // 16], U16, name="offsets")
         nc.sync.dma_start(offsets[:], offs)
         size = held.tile([P, 2 * S], F32, name="size")
-        width = [held.tile([P, S], F32, name=f"width{b}") for b in range(BLOCKS)]
-        centre = [held.tile([P, S], F32, name=f"centre{b}") for b in range(BLOCKS)]
+        raw = [held.tile([P, 2, S], F32, name=f"raw{b}") for b in range(BLOCKS)]
+        centre = [raw[b][:, 0, :] for b in range(BLOCKS)]
+        width = [raw[b][:, 1, :] for b in range(BLOCKS)]
+        by_block = table.rearrange("(t b p) s -> b p t s", t=2, b=BLOCKS, p=P)
         head = [held.tile([P, N], F32, name=f"head{b}") for b in range(BLOCKS)]
         tail = [held.tile([P, N], F32, name=f"tail{b}") for b in range(BLOCKS)]
 
         def load_rows(tile_ap, rows, b, cols):
             nc.sync.dma_start(tile_ap[:, cols], rows[b * P : (b + 1) * P, cols])
 
+
         for turn, b in enumerate(ORDER):
             other = (b + 2) % BLOCKS
             if turn == 0:
                 nc.scalar.dma_start(size[:], box_size.rearrange("h s -> (h s)").partition_broadcast(P))
-                load_rows(width[b], table, BLOCKS + b, slice(0, S))
-                load_rows(centre[b], table, b, slice(0, S))
+                nc.sync.dma_start(width[b], by_block[b][:, 1, :])
+                nc.sync.dma_start(centre[b], by_block[b][:, 0, :])
                 for k in range(PIECES):
                     load_rows(head[b], head_emb, b, slice(k * PIECE, (k + 1) * PIECE))
                     nc.sync.dma_start(
@@ -53,10 +56,9 @@ def tile_boxe_kernel(tc, table, box_size, head_emb, tail_emb, offs, out):
                         tail_emb[other * P : (other + 1) * P, k * PIECE : (k + 1) * PIECE],
                     )
             else:
-                load_rows(centre[b], table, b, slice(0, S))
                 load_rows(head[b], head_emb, b, slice(0, N))
                 nc.sync.dma_start(tail[b][:], tail_emb[other * P : (other + 1) * P, :])
-                load_rows(width[b], table, BLOCKS + b, slice(0, S))
+                nc.sync.dma_start(raw[b][:], by_block[b])
 
         ones_to = held.tile([P, ROWS, ROWS], BF16, name="ones_to")
         nc.gpsimd.memset(ones_to[:], 0.0)
@@ -82,9 +84,9 @@ def tile_boxe_kernel(tc, table, box_size, head_emb, tail_emb, offs, out):
 
         def of_table_alone(b):
             abs_width[b] = held.tile([P, S], F32, name=f"abs_width{b}")
-            nc.scalar.activation(abs_width[b][:], width[b][:], FN.Abs)
+            nc.scalar.activation(abs_width[b][:], width[b], FN.Abs)
             tanh_centre[b] = held.tile([P, S], F32, name=f"tanh_centre{b}")
-            nc.scalar.activation(tanh_centre[b][:], centre[b][:], FN.Tanh)
+            nc.scalar.activation(tanh_centre[b][:], centre[b], FN.Tanh)
 
         def bump(u):
             b, k = ORDER[u // PIECES], u % PIECES

@@ -66,11 +66,9 @@ def tile_boxe_kernel(tc, table, box_size, head_emb, tail_emb, offs, out):
             nc.gpsimd.memset(ones_to[:, q, q : q + 1], 1.0)
         identity = held.tile([P, P], F32, name="identity")
         make_identity(nc, identity[:])
-        minus_identity = held.tile([P, P], F32, name="minus_identity")
-        nc.gpsimd.tensor_scalar(minus_identity[:], identity[:], -1.0, None, ALU.mult)
 
         abs_width, tanh_centre, minus_bumped = {}, {}, {}
-        minus_w, inv_p, minus_gain = {}, {}, {}
+        minus_w, inv_p = {}, {}
 
         below = held.tile([P, 2 * S], F32, name="below")
         scale = held.tile([P, 2 * S], F32, name="scale")
@@ -112,15 +110,11 @@ def tile_boxe_kernel(tc, table, box_size, head_emb, tail_emb, offs, out):
             inv_p[b] = held.tile([P, S], F32, name=f"inv_p{b}")
             nc.scalar.activation(inv_p[b][:], decay[:], FN.Copy, bias=0.5, scale=0.5)
 
-        def gain(b):
-            minus_gain[b] = held.tile([P, S], F32, name=f"minus_gain{b}")
-            nc.vector.scalar_tensor_tensor(minus_gain[b][:], inv_p[b][:], -1.0, minus_w[b][:], ALU.add, ALU.add)
-
         def piece_of(u):
             k = u % PIECES
             return offsets[:, k * (PIECE // 16) : (k + 1) * (PIECE // 16)]
 
-        twice_cd, twice_outside, inner, twice_dist, squared = {}, {}, {}, {}, {}
+        twice_cd, beyond, twice_outside, minus_clipped, minus_inner, minus_twice_dist, squared = {}, {}, {}, {}, {}, {}, {}
         total = [totals.tile([ROWS, CHUNK], F32, name=f"total{box}") for box in range(2)]
         norm = [held.tile([ROWS, CHUNK], F32, name=f"norm{box}") for box in range(2)]
 
@@ -133,27 +127,33 @@ def tile_boxe_kernel(tc, table, box_size, head_emb, tail_emb, offs, out):
 
         def second_stage(u):
             b = ORDER[u // PIECES]
-            beyond = held.tile([P, PIECE], F32, name=f"beyond{u}")
-            nc.vector.tensor_tensor(beyond[:], minus_w[b][:].indirect(piece_of(u)), twice_cd[u][:], ALU.add)
+            beyond[u] = held.tile([P, PIECE], F32, name=f"beyond{u}")
+            nc.vector.tensor_tensor(beyond[u][:], minus_w[b][:].indirect(piece_of(u)), twice_cd[u][:], ALU.add)
             twice_outside[u] = held.tile([P, PIECE], F32, name=f"twice_outside{u}")
-            nc.scalar.activation(twice_outside[u][:], beyond[:], FN.Relu)
-            inner[u] = held.tile([P, PIECE], F32, name=f"inner{u}")
-            nc.vector.tensor_tensor(inner[u][:], inv_p[b][:].indirect(piece_of(u)), twice_cd[u][:], ALU.mult)
-            if u < UNITS - 1:
-                twice_dist[u] = dists.tile([P, PIECE], F32, name="twice_dist")
-                nc.tensor.matmul(twice_dist[u][:], identity[:], inner[u][:], start=True, stop=False)
+            nc.scalar.activation(twice_outside[u][:], beyond[u][:], FN.Relu)
+
+        def clip_stage(u):
+            minus_clipped[u] = held.tile([P, PIECE], F32, name=f"minus_clipped{u}")
+            nc.vector.scalar_tensor_tensor(minus_clipped[u][:], beyond[u][:], 0.0, twice_cd[u][:], ALU.max, ALU.subtract)
 
         def third_stage(u):
             b = ORDER[u // PIECES]
+            minus_inner[u] = held.tile([P, PIECE], F32, name=f"minus_inner{u}")
+            nc.vector.tensor_tensor(minus_inner[u][:], inv_p[b][:].indirect(piece_of(u)), minus_clipped[u][:], ALU.mult)
+            if u < UNITS - 1:
+                minus_twice_dist[u] = dists.tile([P, PIECE], F32, name="minus_twice_dist")
+                nc.tensor.matmul(minus_twice_dist[u][:], identity[:], minus_inner[u][:], start=True, stop=False)
+
+        def outer_stage(u):
             minus_outer = held.tile([P, PIECE], F32, name=f"minus_outer{u}")
-            nc.vector.tensor_tensor(minus_outer[:], minus_gain[b][:].indirect(piece_of(u)), twice_outside[u][:], ALU.mult)
+            nc.vector.scalar_tensor_tensor(minus_outer[:], minus_clipped[u][:], -1.0, twice_outside[u][:], ALU.add, ALU.mult)
             squared[u] = held.tile([P, PIECE], BF16, name=f"squared{u}")
             if u < UNITS - 1:
-                nc.tensor.matmul(twice_dist[u][:], minus_identity[:], minus_outer[:], start=False, stop=True)
-                nc.scalar.activation(squared[u][:], twice_dist[u][:], FN.Square, scale=0.5)
+                nc.tensor.matmul(minus_twice_dist[u][:], identity[:], minus_outer[:], start=False, stop=True)
+                nc.scalar.activation(squared[u][:], minus_twice_dist[u][:], FN.Square, scale=0.5)
             else:
                 last = held.tile([P, PIECE], F32, name="last")
-                nc.vector.tensor_tensor(last[:], inner[u][:], minus_outer[:], ALU.subtract)
+                nc.vector.tensor_tensor(last[:], minus_inner[u][:], minus_outer[:], ALU.add)
                 nc.vector.scalar_tensor_tensor(squared[u][:], last[:], 0.25, last[:], ALU.mult, ALU.mult)
 
         def fourth_stage(u):
@@ -179,17 +179,19 @@ def tile_boxe_kernel(tc, table, box_size, head_emb, tail_emb, offs, out):
         bump(1)
 
         for step in range(UNITS + 3):
+            if 0 <= step - 2 < UNITS:
+                clip_stage(step - 2)
             if step < UNITS:
                 first_stage(step)
             if 0 <= step - 2 < UNITS:
                 third_stage(step - 2)
             if 0 <= step - 1 < UNITS:
                 second_stage(step - 1)
+            if 0 <= step - 2 < UNITS:
+                outer_stage(step - 2)
             if 0 <= step - 3 < UNITS:
                 fourth_stage(step - 3)
             turn, k = step // PIECES, step % PIECES
-            if k == 0 and turn < BLOCKS:
-                gain(ORDER[turn])
             if turn + 1 < BLOCKS:
                 coming = ORDER[turn + 1]
                 if k == 0:

@@ -89,7 +89,7 @@ def tile_boxe_kernel(tc, table, box_size, head_emb, tail_emb, offs, out):
         def bump(u):
             b, k = ORDER[u // PIECES], u % PIECES
             cols = slice(k * PIECE, (k + 1) * PIECE)
-            if u < PIECES:
+            if u < 2 * PIECES:
                 both = held.tile([P, PIECE], F32, name=f"both{u}")
                 nc.vector.tensor_tensor(both[:], head[b][:, cols], tail[b][:, cols], ALU.add)
             else:

@@ -13,7 +13,7 @@ N = 512
 BLOCKS = 4
 PIECE = 256
 PIECES = N // PIECE
-ORDER = (0, 2, 1, 3)
+ORDER = (0, 1, 2, 3)
 UNITS = BLOCKS * PIECES
 ROWS = 4
 CHUNK = N // ROWS
@@ -150,11 +150,14 @@ def tile_boxe_kernel(tc, table, box_size, head_emb, tail_emb, offs, out):
             squared[u] = held.tile([P, PIECE], BF16, name=f"squared{u}")
             if u < UNITS - 1:
                 nc.tensor.matmul(minus_twice_dist[u][:], identity[:], minus_outer[:], start=False, stop=True)
-                nc.scalar.activation(squared[u][:], minus_twice_dist[u][:], FN.Square, scale=0.5)
             else:
                 last = held.tile([P, PIECE], F32, name="last")
                 nc.vector.tensor_tensor(last[:], minus_inner[u][:], minus_outer[:], ALU.add)
                 nc.vector.scalar_tensor_tensor(squared[u][:], last[:], 0.25, last[:], ALU.mult, ALU.mult)
+
+        def square_stage(u):
+            if u < UNITS - 1:
+                nc.scalar.activation(squared[u][:], minus_twice_dist[u][:], FN.Square, scale=0.5)
 
         def fourth_stage(u):
             b, k = ORDER[u // PIECES], u % PIECES
@@ -178,7 +181,7 @@ def tile_boxe_kernel(tc, table, box_size, head_emb, tail_emb, offs, out):
         widths(ORDER[0])
         bump(1)
 
-        for step in range(UNITS + 3):
+        for step in range(UNITS + 5):
             if 0 <= step - 2 < UNITS:
                 clip_stage(step - 2)
             if step < UNITS:
@@ -190,7 +193,9 @@ def tile_boxe_kernel(tc, table, box_size, head_emb, tail_emb, offs, out):
             if 0 <= step - 2 < UNITS:
                 outer_stage(step - 2)
             if 0 <= step - 3 < UNITS:
-                fourth_stage(step - 3)
+                square_stage(step - 3)
+            if 0 <= step - 4 < UNITS:
+                fourth_stage(step - 4)
             turn, k = step // PIECES, step % PIECES
             if turn + 1 < BLOCKS:
                 coming = ORDER[turn + 1]

import concourse.mybir as mybir
from concourse.masks import make_identity

F32 = mybir.dt.float32
BF16 = mybir.dt.bfloat16
U16 = mybir.dt.uint16
FN = mybir.ActivationFunctionType
ALU = mybir.AluOpType

P = 128
S = 256
N = 512
BLOCKS = 4
PIECE = 256
PIECES = N // PIECE
ORDER = (0, 1, 2, 3)
UNITS = BLOCKS * PIECES
ROWS = 4
CHUNK = N // ROWS

FLOPS = 2 * BLOCKS * P * N


def tile_boxe_kernel(tc, table, box_size, head_emb, tail_emb, offs, out):
    nc = tc.nc
    with (
        tc.tile_pool(name="held", bufs=1) as held,
        tc.psum_pool(name="totals", bufs=1) as totals,
        tc.psum_pool(name="sums", bufs=2) as sums,
        tc.psum_pool(name="dists", bufs=4) as dists,
    ):
        offsets = held.tile([P, N // 16], U16, name="offsets")
        nc.sync.dma_start(offsets[:], offs)
        size = held.tile([P, 2 * S], F32, name="size")
        raw = [held.tile([P, 2, S], F32, name=f"raw{b}") for b in range(BLOCKS)]
        centre = [raw[b][:, 0, :] for b in range(BLOCKS)]
        width = [raw[b][:, 1, :] for b in range(BLOCKS)]
        by_block = table.rearrange("(t b p) s -> b p t s", t=2, b=BLOCKS, p=P)
        head = [held.tile([P, N], F32, name=f"head{b}") for b in range(BLOCKS)]
        tail = [held.tile([P, N], F32, name=f"tail{b}") for b in range(BLOCKS)]

        def load_rows(tile_ap, rows, b, cols):
            nc.sync.dma_start(tile_ap[:, cols], rows[b * P : (b + 1) * P, cols])


        for turn, b in enumerate(ORDER):
            other = (b + 2) % BLOCKS
            if turn == 0:
                nc.scalar.dma_start(size[:], box_size.rearrange("h s -> (h s)").partition_broadcast(P))
                nc.sync.dma_start(width[b], by_block[b][:, 1, :])
                nc.sync.dma_start(centre[b], by_block[b][:, 0, :])
                for k in range(PIECES):
                    load_rows(head[b], head_emb, b, slice(k * PIECE, (k + 1) * PIECE))
                    nc.sync.dma_start(
                        tail[b][:, k * PIECE : (k + 1) * PIECE],
                        tail_emb[other * P : (other + 1) * P, k * PIECE : (k + 1) * PIECE],
                    )
            else:
                load_rows(head[b], head_emb, b, slice(0, N))
                nc.sync.dma_start(tail[b][:], tail_emb[other * P : (other + 1) * P, :])
                nc.sync.dma_start(raw[b][:], by_block[b])

        ones_to = held.tile([P, ROWS, ROWS], BF16, name="ones_to")
        nc.gpsimd.memset(ones_to[:], 0.0)
        for q in range(ROWS):
            nc.gpsimd.memset(ones_to[:, q, q : q + 1], 1.0)
        identity = held.tile([P, P], F32, name="identity")
        make_identity(nc, identity[:])

        abs_width, tanh_centre, minus_bumped = {}, {}, {}
        minus_w, inv_p = {}, {}

        below = held.tile([P, 2 * S], F32, name="below")
        scale = held.tile([P, 2 * S], F32, name="scale")

        def start_scale():
            nc.vector.tensor_scalar_min(below[:], size[:], 0.0)
            nc.scalar.activation(below[:], below[:], FN.Exp)

        def end_scale():
            nc.vector.scalar_tensor_tensor(scale[:], size[:], 0.0, below[:], ALU.max, ALU.add)

        def of_table_alone(b):
            abs_width[b] = held.tile([P, S], F32, name=f"abs_width{b}")
            nc.scalar.activation(abs_width[b][:], width[b], FN.Abs)
            tanh_centre[b] = held.tile([P, S], F32, name=f"tanh_centre{b}")
            nc.scalar.activation(tanh_centre[b][:], centre[b], FN.Tanh)

        def bump(u):
            b, k = ORDER[u // PIECES], u % PIECES
            cols = slice(k * PIECE, (k + 1) * PIECE)
            if u < 2 * PIECES:
                both = held.tile([P, PIECE], F32, name=f"both{u}")
                nc.vector.tensor_tensor(both[:], head[b][:, cols], tail[b][:, cols], ALU.add)
            else:
                both = sums.tile([P, PIECE], F32, name="both")
                nc.tensor.matmul(both[:], identity[:], head[b][:, cols], start=True, stop=False)
                nc.tensor.matmul(both[:], identity[:], tail[b][:, cols], start=False, stop=True)
            minus_bumped[u] = held.tile([P, PIECE], F32, name=f"minus_bumped{u}")
            nc.scalar.activation(minus_bumped[u][:], both[:], FN.Tanh, scale=-1.0)

        def widths(b):
            arg = held.tile([P, S], F32, name=f"arg{b}")
            box = b // 2
            nc.vector.tensor_tensor(arg[:], abs_width[b][:], scale[:, box * S : (box + 1) * S], ALU.mult)
            minus_w[b] = held.tile([P, S], F32, name=f"minus_w{b}")
            nc.scalar.activation(minus_w[b][:], arg[:], FN.Tanh, scale=-1.0)
            decay = held.tile([P, S], F32, name=f"decay{b}")
            nc.scalar.activation(decay[:], arg[:], FN.Exp, scale=-2.0)
            inv_p[b] = held.tile([P, S], F32, name=f"inv_p{b}")
            nc.scalar.activation(inv_p[b][:], decay[:], FN.Copy, bias=0.5, scale=0.5)

        def piece_of(u):
            k = u % PIECES
            return offsets[:, k * (PIECE // 16) : (k + 1) * (PIECE // 16)]

        twice_cd, beyond, twice_outside, minus_clipped, minus_inner, minus_twice_dist, squared = {}, {}, {}, {}, {}, {}, {}
        total = [totals.tile([ROWS, CHUNK], F32, name=f"total{box}") for box in range(2)]
        norm = [held.tile([ROWS, CHUNK], F32, name=f"norm{box}") for box in range(2)]

        def first_stage(u):
            b = ORDER[u // PIECES]
            diff = held.tile([P, PIECE], F32, name=f"diff{u}")
            nc.vector.tensor_tensor(diff[:], tanh_centre[b][:].indirect(piece_of(u)), minus_bumped[u][:], ALU.add)
            twice_cd[u] = held.tile([P, PIECE], F32, name=f"twice_cd{u}")
            nc.scalar.activation(twice_cd[u][:], diff[:], FN.Abs, scale=2.0)

        def second_stage(u):
            b = ORDER[u // PIECES]
            beyond[u] = held.tile([P, PIECE], F32, name=f"beyond{u}")
            nc.vector.tensor_tensor(beyond[u][:], minus_w[b][:].indirect(piece_of(u)), twice_cd[u][:], ALU.add)
            twice_outside[u] = held.tile([P, PIECE], F32, name=f"twice_outside{u}")
            nc.scalar.activation(twice_outside[u][:], beyond[u][:], FN.Relu)

        def clip_stage(u):
            minus_clipped[u] = held.tile([P, PIECE], F32, name=f"minus_clipped{u}")
            nc.vector.scalar_tensor_tensor(minus_clipped[u][:], beyond[u][:], 0.0, twice_cd[u][:], ALU.max, ALU.subtract)

        def third_stage(u):
            b = ORDER[u // PIECES]
            minus_inner[u] = held.tile([P, PIECE], F32, name=f"minus_inner{u}")
            nc.vector.tensor_tensor(minus_inner[u][:], inv_p[b][:].indirect(piece_of(u)), minus_clipped[u][:], ALU.mult)
            if u < UNITS - 1:
                minus_twice_dist[u] = dists.tile([P, PIECE], F32, name="minus_twice_dist")
                nc.tensor.matmul(minus_twice_dist[u][:], identity[:], minus_inner[u][:], start=True, stop=False)

        def outer_stage(u):
            minus_outer = held.tile([P, PIECE], F32, name=f"minus_outer{u}")
            nc.vector.scalar_tensor_tensor(minus_outer[:], minus_clipped[u][:], -1.0, twice_outside[u][:], ALU.add, ALU.mult)
            squared[u] = held.tile([P, PIECE], BF16, name=f"squared{u}")
            if u < UNITS - 1:
                nc.tensor.matmul(minus_twice_dist[u][:], identity[:], minus_outer[:], start=False, stop=True)
            else:
                last = held.tile([P, PIECE], F32, name="last")
                nc.vector.tensor_tensor(last[:], minus_inner[u][:], minus_outer[:], ALU.add)
                nc.vector.scalar_tensor_tensor(squared[u][:], last[:], 0.25, last[:], ALU.mult, ALU.mult)

        def square_stage(u):
            if u < UNITS - 1:
                nc.scalar.activation(squared[u][:], minus_twice_dist[u][:], FN.Square, scale=0.5)

        def fourth_stage(u):
            b, k = ORDER[u // PIECES], u % PIECES
            box = b // 2
            for half in range(PIECE // CHUNK):
                q = k * (PIECE // CHUNK) + half
                nc.tensor.matmul(
                    total[box][:],
                    ones_to[:, q, :],
                    squared[u][:, half * CHUNK : (half + 1) * CHUNK],
                    start=(b % 2 == 0 and q == 0),
                    stop=(b % 2 == 1 and q == ROWS - 1),
                )
            if b % 2 == 1 and k == PIECES - 1:
                nc.scalar.activation(norm[box][:], total[box][:], FN.Sqrt)

        start_scale()
        of_table_alone(ORDER[0])
        end_scale()
        bump(0)
        widths(ORDER[0])
        bump(1)

        for step in range(UNITS + 5):
            if 0 <= step - 2 < UNITS:
                clip_stage(step - 2)
            if step < UNITS:
                first_stage(step)
            if 0 <= step - 2 < UNITS:
                third_stage(step - 2)
            if 0 <= step - 1 < UNITS:
                second_stage(step - 1)
            if 0 <= step - 2 < UNITS:
                outer_stage(step - 2)
            if 0 <= step - 3 < UNITS:
                square_stage(step - 3)
            if 0 <= step - 4 < UNITS:
                fourth_stage(step - 4)
            turn, k = step // PIECES, step % PIECES
            if turn + 1 < BLOCKS:
                coming = ORDER[turn + 1]
                if k == 0:
                    of_table_alone(coming)
                    for u in range(PIECES * (turn + 1), PIECES * (turn + 2)):
                        bump(u)
                else:
                    widths(coming)

        score = held.tile([ROWS, CHUNK], F32, name="score")
        nc.vector.scalar_tensor_tensor(score[:], norm[0][:], -1.0, norm[1][:], ALU.mult, ALU.subtract)
        nc.sync.dma_start(out.rearrange("o (q n) -> (o q) n", q=ROWS), score[:])
